import numpy as np
import ml_dtypes


def mxq(x, axis, fmt="e4m3"):
    dtype, down = {"e4m3": (ml_dtypes.float8_e4m3fn, 7), "e5m2": (ml_dtypes.float8_e5m2, 14)}[fmt]
    v = np.moveaxis(np.asarray(x, np.float32).astype(ml_dtypes.bfloat16).astype(np.float64), axis, -1)
    blocks = v.reshape(v.shape[:-1] + (-1, 32))
    amax = np.abs(blocks).max(-1, keepdims=True)
    byte = np.maximum(np.where(amax > 0, np.frexp(amax)[1] - 1 + 127, 0) - down, 1)
    scale = np.exp2(byte - 127.0)
    codes = (blocks / scale).astype(np.float32).astype(dtype).astype(np.float64)
    return np.moveaxis((codes * scale).reshape(v.shape), -1, axis)


WIDE = False


def mx_kscale(k):
    if not WIDE:
        return np.ones(k)
    levels = np.array([20, -20, 10, -10, 0])
    a = np.random.permutation(np.resize(levels, k // 512 * 4)).reshape(k // 512, 4)
    idx = np.arange(k)
    return np.exp2(a[idx // 512, idx % 128 // 32])


BF16 = ml_dtypes.bfloat16


def bf(x):
    return np.asarray(x, np.float32).astype(BF16)


def f64(x):
    return np.asarray(x).astype(np.float64)


B, O, A, H, Z = 1024, 512, 512, 512, 512
I = O + Z + A


def sigmoid(v):
    return 1.0 / (1.0 + np.exp(-v))


def setup_inputs():
    s = mx_kscale(B)[:, None]
    x0 = bf(np.random.standard_normal((B, O)))
    z0 = bf(np.random.standard_normal((B, Z)) * 1.4)
    a0 = bf(np.random.standard_normal((B, A)))
    h_prev = bf(np.random.standard_normal((B, H)))
    w_ih = bf(np.random.standard_normal((3 * H, I)) / np.sqrt(I))
    w_hh = bf(np.random.standard_normal((3 * H, H)) / np.sqrt(H))
    b_ih = bf(np.random.standard_normal(3 * H) * 0.2)
    b_hh = bf(np.random.standard_normal(3 * H) * 0.2)
    g = bf(np.random.standard_normal((B, H)) * 4.0 * np.exp2(np.random.randint(-12, 1, (B, 1))) / s)
    u0 = np.concatenate([f64(x0), f64(z0), f64(a0)], -1)
    gi = u0 @ f64(w_ih).T + f64(b_ih)
    gh = f64(h_prev) @ f64(w_hh).T + f64(b_hh)
    r = sigmoid(gi[:, :H] + gh[:, :H])
    zg = sigmoid(gi[:, H:2 * H] + gh[:, H:2 * H])
    hn = gh[:, 2 * H:]
    n = np.tanh(gi[:, 2 * H:] + r * hn)
    gates = np.concatenate([r, zg, n], -1)
    return {
        "x_t": bf(f64(x0) * s),
        "z_t": bf(f64(z0) * s),
        "a_prev": bf(f64(a0) * s),
        "h_prev": h_prev,
        "w_ih": w_ih,
        "w_hh": w_hh,
        "b_ih": b_ih,
        "b_hh": b_hh,
        "gates": np.asarray(gates, np.float32),
        "h_n": np.asarray(hn, np.float32),
        "grad_out": g,
    }


def reference(x_t, z_t, a_prev, h_prev, w_ih, w_hh, b_ih, b_hh, gates, h_n, grad_out):
    g = f64(grad_out)
    gt = f64(gates)
    r, zg, n = gt[:, :H], gt[:, H:2 * H], gt[:, 2 * H:]
    d_n = g * (1.0 - zg) * (1.0 - n * n)
    d_r = d_n * f64(h_n) * r * (1.0 - r)
    d_z = g * (f64(h_prev) - n) * zg * (1.0 - zg)
    dgi = np.concatenate([d_r, d_z, d_n], -1)
    u = np.concatenate([f64(x_t), f64(z_t), f64(a_prev)], -1)
    return mxq(dgi, 0, "e5m2").T @ mxq(u, 0, "e4m3")

@@ -1,0 +1,190 @@
+from contextlib import ExitStack
+
+import concourse.mybir as mybir
+
+F32 = mybir.dt.float32
+BF16 = mybir.dt.bfloat16
+U32 = mybir.dt.uint32
+U8 = mybir.dt.uint8
+E4M3_X4 = mybir.dt.float8_e4m3fn_x4
+E5M2_X4 = mybir.dt.float8_e5m2_x4
+ALU = mybir.AluOpType
+ACT = mybir.ActivationFunctionType
+
+P = 128
+PACK = 4
+K_PASS = P * PACK
+TOKENS = 1024
+PASSES = TOKENS // K_PASS
+H = 512
+GATES = 3
+STREAMS = 3
+M_TILE = 128
+TILES_PER_GATE = H // M_TILE
+RUN = 4
+
+FLOPS = 2 * TOKENS * (GATES * H) * (STREAMS * H)
+BYTES = 2 * 5 * TOKENS * H + 4 * (GATES + 1) * TOKENS * H + 4 * (GATES * H) * (STREAMS * H)
+
+
+def tokens_by_pass(dram):
+    return dram.rearrange("(s p j) w -> s p j w", s=PASSES, p=P, j=PACK)
+
+
+def tile_vrnncell_pc_v_kernel(
+    tc, x_t, z_t, a_prev, h_prev, w_ih, w_hh, b_ih, b_hh, gates, h_n, grad_out, out
+):
+    nc = tc.nc
+    with ExitStack() as ctx:
+        keep = ctx.enter_context(tc.tile_pool(name="keep", bufs=1))
+        group = ctx.enter_context(tc.tile_pool(name="group", bufs=3))
+        stage = ctx.enter_context(tc.tile_pool(name="stage", bufs=5))
+        psum = ctx.enter_context(tc.psum_pool(name="psum", bufs=8))
+
+        whole = [P, PASSES, PACK, H]
+        g_sb = keep.tile(whole, BF16)
+        h_sb = keep.tile(whole, BF16)
+        x_sb = keep.tile(whole, BF16)
+        z_sb = keep.tile(whole, BF16)
+        a_sb = keep.tile(whole, BF16)
+        r_sb = keep.tile(whole, F32)
+        zg_sb = keep.tile(whole, F32)
+        n_sb = keep.tile(whole, F32)
+        hn_sb = keep.tile(whole, F32)
+        neg_ga = keep.tile(whole, F32)
+        d_n = keep.tile(whole, F32)
+
+        dgi_codes = keep.tile([P, GATES * TILES_PER_GATE, PASSES, M_TILE], U32, align_bytes=64)
+        dgi_scales = keep.tile([P, GATES * TILES_PER_GATE, PASSES, M_TILE], U8, align_bytes=64)
+        u_codes = keep.tile([P, PASSES, STREAMS * H], U32, align_bytes=64)
+        u_scales = keep.tile([P, PASSES, STREAMS * H], U8, align_bytes=64)
+
+        def load(tile, dram, s):
+            nc.sync.dma_start(out=tile[:, s], in_=tokens_by_pass(dram)[s])
+
+        r_dram = gates[:, 0 * H : 1 * H]
+        zg_dram = gates[:, 1 * H : 2 * H]
+        n_dram = gates[:, 2 * H : 3 * H]
+
+        load(g_sb, grad_out, 0)
+        load(zg_sb, zg_dram, 0)
+        load(x_sb, x_t, 0)
+        load(n_sb, n_dram, 0)
+        load(x_sb, x_t, 1)
+        load(g_sb, grad_out, 1)
+        load(zg_sb, zg_dram, 1)
+        load(z_sb, z_t, 0)
+        load(n_sb, n_dram, 1)
+        load(z_sb, z_t, 1)
+        load(a_sb, a_prev, 0)
+        load(a_sb, a_prev, 1)
+        for s in range(PASSES):
+            load(h_sb, h_prev, s)
+        for s in range(PASSES):
+            load(r_sb, r_dram, s)
+        for s in range(PASSES):
+            load(hn_sb, h_n, s)
+
+        def rows_side_by_side(dst, src):
+            nc.scalar.copy(
+                out=dst.rearrange("p (c i) j -> p c j i", i=RUN),
+                in_=src.rearrange("p j (c i) -> p c j i", i=RUN),
+            )
+
+        def quantise_stream(i, tile, s):
+            grouped = group.tile([P, H, PACK], BF16, align_bytes=64, tag="wide")
+            rows_side_by_side(grouped[:], tile[:, s])
+            nc.vector.quantize_mx(
+                out=u_codes[:, s, i * H : (i + 1) * H].bitcast(E4M3_X4),
+                scales=u_scales[:, s, i * H : (i + 1) * H],
+                in_=grouped[:].rearrange("p w j -> p (w j)"),
+            )
+
+        def make_d_n(s):
+            nc.vector.scalar_tensor_tensor(
+                out=neg_ga[:, s], in0=zg_sb[:, s], scalar=1.0, in1=g_sb[:, s],
+                op0=ALU.subtract, op1=ALU.mult,
+            )
+            nc.vector.tensor_tensor(out=zg_sb[:, s], in0=neg_ga[:, s], in1=zg_sb[:, s], op=ALU.mult)
+            nc.scalar.activation(out=d_n[:, s], in_=n_sb[:, s], func=ACT.Square)
+            nc.vector.scalar_tensor_tensor(
+                out=d_n[:, s], in0=d_n[:, s], scalar=1.0, in1=neg_ga[:, s],
+                op0=ALU.subtract, op1=ALU.mult,
+            )
+            grouped = group.tile([P, H, PACK], BF16, align_bytes=64, tag="wide")
+            rows_side_by_side(grouped[:], d_n[:, s])
+            for b in range(TILES_PER_GATE):
+                m = 2 * TILES_PER_GATE + b
+                nc.vector.quantize_mx(
+                    out=dgi_codes[:, m, s, :].bitcast(E5M2_X4),
+                    scales=dgi_scales[:, m, s, :],
+                    in_=grouped[:, b * M_TILE : (b + 1) * M_TILE, :].rearrange("p w j -> p (w j)"),
+                )
+
+        def quantise_tile(m, factor0, factor1):
+            grouped = group.tile([P, PASSES, M_TILE, PACK], BF16, align_bytes=64, tag="narrow")
+            nc.vector.tensor_tensor(
+                out=grouped[:],
+                in0=factor0.rearrange("p s j w -> p s w j"),
+                in1=factor1.rearrange("p s j w -> p s w j"),
+                op=ALU.mult,
+            )
+            nc.vector.quantize_mx(
+                out=dgi_codes[:, m].rearrange("p s w -> p (s w)").bitcast(E5M2_X4),
+                scales=dgi_scales[:, m].rearrange("p s w -> p (s w)"),
+                in_=grouped[:].rearrange("p s w j -> p (s w j)"),
+            )
+
+        def make_d_z(b):
+            cols = slice(b * M_TILE, (b + 1) * M_TILE)
+            nc.vector.tensor_tensor(
+                out=n_sb[:, :, :, cols], in0=n_sb[:, :, :, cols], in1=h_sb[:, :, :, cols],
+                op=ALU.subtract,
+            )
+            quantise_tile(1 * TILES_PER_GATE + b, n_sb[:, :, :, cols], zg_sb[:, :, :, cols])
+
+        def make_d_r(b):
+            cols = slice(b * M_TILE, (b + 1) * M_TILE)
+            nc.vector.scalar_tensor_tensor(
+                out=r_sb[:, :, :, cols], in0=r_sb[:, :, :, cols], scalar=1.0,
+                in1=r_sb[:, :, :, cols], op0=ALU.subtract, op1=ALU.mult,
+            )
+            nc.vector.scalar_tensor_tensor(
+                out=r_sb[:, :, :, cols], in0=r_sb[:, :, :, cols], scalar=-1.0,
+                in1=hn_sb[:, :, :, cols], op0=ALU.mult, op1=ALU.mult,
+            )
+            quantise_tile(0 * TILES_PER_GATE + b, r_sb[:, :, :, cols], d_n[:, :, :, cols])
+
+        def multiply_rows(m):
+            rows = stage.tile([P, STREAMS * H], F32)
+            for i in range(STREAMS):
+                acc = psum.tile([P, H], F32)
+                for s in range(PASSES):
+                    nc.tensor.matmul_mx(
+                        out=acc[:],
+                        lhsT=dgi_codes[:, m, s, :].bitcast(E5M2_X4),
+                        lhsT_scale=dgi_scales[:, m, s, :],
+                        rhs=u_codes[:, s, i * H : (i + 1) * H].bitcast(E4M3_X4),
+                        rhs_scale=u_scales[:, s, i * H : (i + 1) * H],
+                        start=(s == 0),
+                        stop=(s == PASSES - 1),
+                    )
+                nc.scalar.copy(out=rows[:, i * H : (i + 1) * H], in_=acc[:])
+            nc.sync.dma_start(out=out[m * M_TILE : (m + 1) * M_TILE, :], in_=rows[:])
+
+        quantise_stream(0, x_sb, 0)
+        make_d_n(0)
+        quantise_stream(0, x_sb, 1)
+        quantise_stream(1, z_sb, 0)
+        make_d_n(1)
+        quantise_stream(1, z_sb, 1)
+        quantise_stream(2, a_sb, 0)
+        quantise_stream(2, a_sb, 1)
+        for b in range(TILES_PER_GATE):
+            multiply_rows(2 * TILES_PER_GATE + b)
+        for b in range(TILES_PER_GATE):
+            make_d_z(b)
+            multiply_rows(1 * TILES_PER_GATE + b)
+        for b in range(TILES_PER_GATE):
+            make_d_r(b)
+            multiply_rows(0 * TILES_PER_GATE + b)

@@ -1,6 +1,7 @@
 from contextlib import ExitStack
 
 import concourse.mybir as mybir
+from concourse.masks import make_identity
 
 F32 = mybir.dt.float32
 BF16 = mybir.dt.bfloat16
@@ -37,7 +38,7 @@ def tile_vrnncell_pc_v_kernel(
     nc = tc.nc
     with ExitStack() as ctx:
         keep = ctx.enter_context(tc.tile_pool(name="keep", bufs=1))
-        group = ctx.enter_context(tc.tile_pool(name="group", bufs=3))
+        group = ctx.enter_context(tc.tile_pool(name="group", bufs=4))
         stage = ctx.enter_context(tc.tile_pool(name="stage", bufs=5))
         psum = ctx.enter_context(tc.psum_pool(name="psum", bufs=8))
 
@@ -53,6 +54,9 @@ def tile_vrnncell_pc_v_kernel(
         hn_sb = keep.tile(whole, F32)
         neg_ga = keep.tile(whole, F32)
         d_n = keep.tile(whole, F32)
+        d_z_grouped = keep.tile([P, TILES_PER_GATE, PASSES, M_TILE, PACK], BF16, align_bytes=64)
+        ident = keep.tile([P, P], F32)
+        neg_ident = keep.tile([P, P], BF16)
 
         dgi_codes = keep.tile([P, GATES * TILES_PER_GATE, PASSES, M_TILE], U32, align_bytes=64)
         dgi_scales = keep.tile([P, GATES * TILES_PER_GATE, PASSES, M_TILE], U8, align_bytes=64)
@@ -65,25 +69,13 @@ def tile_vrnncell_pc_v_kernel(
         r_dram = gates[:, 0 * H : 1 * H]
         zg_dram = gates[:, 1 * H : 2 * H]
         n_dram = gates[:, 2 * H : 3 * H]
+        streams = [(x_sb, x_t), (z_sb, z_t), (a_sb, a_prev)]
+        chunks_per_round = STREAMS
+        u_grouped = {}
 
-        load(g_sb, grad_out, 0)
-        load(zg_sb, zg_dram, 0)
-        load(x_sb, x_t, 0)
-        load(n_sb, n_dram, 0)
-        load(x_sb, x_t, 1)
-        load(g_sb, grad_out, 1)
-        load(zg_sb, zg_dram, 1)
-        load(z_sb, z_t, 0)
-        load(n_sb, n_dram, 1)
-        load(z_sb, z_t, 1)
-        load(a_sb, a_prev, 0)
-        load(a_sb, a_prev, 1)
-        for s in range(PASSES):
-            load(h_sb, h_prev, s)
-        for s in range(PASSES):
-            load(r_sb, r_dram, s)
-        for s in range(PASSES):
-            load(hn_sb, h_n, s)
+        def load_chunk(k):
+            tile, dram = streams[k // PASSES]
+            load(tile, dram, k % PASSES)
 
         def rows_side_by_side(dst, src):
             nc.scalar.copy(
@@ -91,74 +83,23 @@ def tile_vrnncell_pc_v_kernel(
                 in_=src.rearrange("p j (c i) -> p c j i", i=RUN),
             )
 
-        def quantise_stream(i, tile, s):
-            grouped = group.tile([P, H, PACK], BF16, align_bytes=64, tag="wide")
-            rows_side_by_side(grouped[:], tile[:, s])
+        def regroup_chunk(k):
+            tile, dram = streams[k // PASSES]
+            u_grouped[k] = group.tile([P, H, PACK], BF16, align_bytes=64, tag="wide", name="u_grouped")
+            rows_side_by_side(u_grouped[k][:], tile[:, k % PASSES])
+
+        def quantise_chunk(k):
+            i, s = k // PASSES, k % PASSES
             nc.vector.quantize_mx(
                 out=u_codes[:, s, i * H : (i + 1) * H].bitcast(E4M3_X4),
                 scales=u_scales[:, s, i * H : (i + 1) * H],
-                in_=grouped[:].rearrange("p w j -> p (w j)"),
+                in_=u_grouped[k][:].rearrange("p w j -> p (w j)"),
             )
-
-        def make_d_n(s):
-            nc.vector.scalar_tensor_tensor(
-                out=neg_ga[:, s], in0=zg_sb[:, s], scalar=1.0, in1=g_sb[:, s],
-                op0=ALU.subtract, op1=ALU.mult,
-            )
-            nc.vector.tensor_tensor(out=zg_sb[:, s], in0=neg_ga[:, s], in1=zg_sb[:, s], op=ALU.mult)
-            nc.scalar.activation(out=d_n[:, s], in_=n_sb[:, s], func=ACT.Square)
-            nc.vector.scalar_tensor_tensor(
-                out=d_n[:, s], in0=d_n[:, s], scalar=1.0, in1=neg_ga[:, s],
-                op0=ALU.subtract, op1=ALU.mult,
-            )
-            grouped = group.tile([P, H, PACK], BF16, align_bytes=64, tag="wide")
-            rows_side_by_side(grouped[:], d_n[:, s])
-            for b in range(TILES_PER_GATE):
-                m = 2 * TILES_PER_GATE + b
-                nc.vector.quantize_mx(
-                    out=dgi_codes[:, m, s, :].bitcast(E5M2_X4),
-                    scales=dgi_scales[:, m, s, :],
-                    in_=grouped[:, b * M_TILE : (b + 1) * M_TILE, :].rearrange("p w j -> p (w j)"),
-                )
-
-        def quantise_tile(m, factor0, factor1):
-            grouped = group.tile([P, PASSES, M_TILE, PACK], BF16, align_bytes=64, tag="narrow")
-            nc.vector.tensor_tensor(
-                out=grouped[:],
-                in0=factor0.rearrange("p s j w -> p s w j"),
-                in1=factor1.rearrange("p s j w -> p s w j"),
-                op=ALU.mult,
-            )
-            nc.vector.quantize_mx(
-                out=dgi_codes[:, m].rearrange("p s w -> p (s w)").bitcast(E5M2_X4),
-                scales=dgi_scales[:, m].rearrange("p s w -> p (s w)"),
-                in_=grouped[:].rearrange("p s w j -> p (s w j)"),
-            )
-
-        def make_d_z(b):
-            cols = slice(b * M_TILE, (b + 1) * M_TILE)
-            nc.vector.tensor_tensor(
-                out=n_sb[:, :, :, cols], in0=n_sb[:, :, :, cols], in1=h_sb[:, :, :, cols],
-                op=ALU.subtract,
-            )
-            quantise_tile(1 * TILES_PER_GATE + b, n_sb[:, :, :, cols], zg_sb[:, :, :, cols])
-
-        def make_d_r(b):
-            cols = slice(b * M_TILE, (b + 1) * M_TILE)
-            nc.vector.scalar_tensor_tensor(
-                out=r_sb[:, :, :, cols], in0=r_sb[:, :, :, cols], scalar=1.0,
-                in1=r_sb[:, :, :, cols], op0=ALU.subtract, op1=ALU.mult,
-            )
-            nc.vector.scalar_tensor_tensor(
-                out=r_sb[:, :, :, cols], in0=r_sb[:, :, :, cols], scalar=-1.0,
-                in1=hn_sb[:, :, :, cols], op0=ALU.mult, op1=ALU.mult,
-            )
-            quantise_tile(0 * TILES_PER_GATE + b, r_sb[:, :, :, cols], d_n[:, :, :, cols])
 
         def multiply_rows(m):
             rows = stage.tile([P, STREAMS * H], F32)
             for i in range(STREAMS):
-                acc = psum.tile([P, H], F32)
+                acc = psum.tile([P, H], F32, tag="acc")
                 for s in range(PASSES):
                     nc.tensor.matmul_mx(
                         out=acc[:],
@@ -172,19 +113,118 @@ def tile_vrnncell_pc_v_kernel(
                 nc.scalar.copy(out=rows[:, i * H : (i + 1) * H], in_=acc[:])
             nc.sync.dma_start(out=out[m * M_TILE : (m + 1) * M_TILE, :], in_=rows[:])
 
-        quantise_stream(0, x_sb, 0)
-        make_d_n(0)
-        quantise_stream(0, x_sb, 1)
-        quantise_stream(1, z_sb, 0)
-        make_d_n(1)
-        quantise_stream(1, z_sb, 1)
-        quantise_stream(2, a_sb, 0)
-        quantise_stream(2, a_sb, 1)
-        for b in range(TILES_PER_GATE):
-            multiply_rows(2 * TILES_PER_GATE + b)
-        for b in range(TILES_PER_GATE):
-            make_d_z(b)
-            multiply_rows(1 * TILES_PER_GATE + b)
-        for b in range(TILES_PER_GATE):
-            make_d_r(b)
-            multiply_rows(0 * TILES_PER_GATE + b)
+        def product_of(factor0, factor1, b):
+            cols = slice(b * M_TILE, (b + 1) * M_TILE)
+            grouped = group.tile([P, PASSES, M_TILE, PACK], BF16, align_bytes=64, tag="narrow")
+            nc.vector.tensor_tensor(
+                out=grouped[:],
+                in0=factor0[:, :, :, cols].rearrange("p s j w -> p s w j"),
+                in1=factor1[:, :, :, cols].rearrange("p s j w -> p s w j"),
+                op=ALU.mult,
+            )
+            return grouped
+
+        def quantise_tile(m, grouped):
+            nc.vector.quantize_mx(
+                out=dgi_codes[:, m].rearrange("p s w -> p (s w)").bitcast(E5M2_X4),
+                scales=dgi_scales[:, m].rearrange("p s w -> p (s w)"),
+                in_=grouped.rearrange("p s w j -> p (s w j)"),
+            )
+
+        def r_slope(b):
+            cols = slice(b * M_TILE, (b + 1) * M_TILE)
+            nc.vector.scalar_tensor_tensor(
+                out=r_sb[:, :, :, cols], in0=r_sb[:, :, :, cols], scalar=1.0,
+                in1=r_sb[:, :, :, cols], op0=ALU.subtract, op1=ALU.mult,
+            )
+
+        def times_h_n(b):
+            cols = slice(b * M_TILE, (b + 1) * M_TILE)
+            nc.vector.scalar_tensor_tensor(
+                out=r_sb[:, :, :, cols], in0=r_sb[:, :, :, cols], scalar=-1.0,
+                in1=hn_sb[:, :, :, cols], op0=ALU.mult, op1=ALU.mult,
+            )
+
+        with tc.manual_schedule():
+            make_identity(nc, ident[:])
+            nc.scalar.mul(out=neg_ident[:], in_=ident[:], mul=-1.0)
+            for s in range(PASSES):
+                first = s * chunks_per_round
+                load(g_sb, grad_out, s)
+                load(zg_sb, zg_dram, s)
+                load_chunk(first)
+                load(n_sb, n_dram, s)
+                load(h_sb, h_prev, s)
+                load_chunk(first + 1)
+                load_chunk(first + 2)
+            for s in range(PASSES):
+                load(r_sb, r_dram, s)
+            for s in range(PASSES):
+                load(hn_sb, h_n, s)
+
+            for s in range(PASSES):
+                first = s * chunks_per_round
+                nc.vector.scalar_tensor_tensor(
+                    out=neg_ga[:, s], in0=zg_sb[:, s], scalar=1.0, in1=g_sb[:, s],
+                    op0=ALU.subtract, op1=ALU.mult,
+                )
+                if s > 0:
+                    quantise_chunk(first - 1)
+                regroup_chunk(first)
+                nc.vector.tensor_tensor(
+                    out=zg_sb[:, s], in0=neg_ga[:, s], in1=zg_sb[:, s], op=ALU.mult
+                )
+                nc.scalar.activation(out=d_n[:, s], in_=n_sb[:, s], func=ACT.Square)
+                regroup_chunk(first + 1)
+                nc.vector.scalar_tensor_tensor(
+                    out=d_n[:, s], in0=d_n[:, s], scalar=1.0, in1=neg_ga[:, s],
+                    op0=ALU.subtract, op1=ALU.mult,
+                )
+                d_n_grouped = group.tile([P, H, PACK], BF16, align_bytes=64, tag="wide")
+                rows_side_by_side(d_n_grouped[:], d_n[:, s])
+                regroup_chunk(first + 2)
+                for b in range(TILES_PER_GATE):
+                    cols = slice(b * M_TILE, (b + 1) * M_TILE)
+                    n_minus_h = psum.tile([P, PACK, M_TILE], F32, tag="acc")
+                    nc.tensor.matmul(
+                        out=n_minus_h[:], lhsT=ident[:], rhs=n_sb[:, s, :, cols],
+                        start=True, stop=False,
+                    )
+                    nc.tensor.matmul(
+                        out=n_minus_h[:], lhsT=neg_ident[:], rhs=h_sb[:, s, :, cols],
+                        start=False, stop=True,
+                    )
+                    nc.vector.tensor_tensor(
+                        out=d_z_grouped[:, b, s],
+                        in0=n_minus_h[:].rearrange("p j w -> p w j"),
+                        in1=zg_sb[:, s, :, cols].rearrange("p j w -> p w j"),
+                        op=ALU.mult,
+                    )
+                quantise_chunk(first)
+                quantise_chunk(first + 1)
+                for b in range(TILES_PER_GATE):
+                    nc.vector.quantize_mx(
+                        out=dgi_codes[:, 2 * TILES_PER_GATE + b, s, :].bitcast(E5M2_X4),
+                        scales=dgi_scales[:, 2 * TILES_PER_GATE + b, s, :],
+                        in_=d_n_grouped[:, b * M_TILE : (b + 1) * M_TILE, :].rearrange(
+                            "p w j -> p (w j)"
+                        ),
+                    )
+            quantise_chunk(PASSES * chunks_per_round - 1)
+
+            for b in range(TILES_PER_GATE):
+                multiply_rows(2 * TILES_PER_GATE + b)
+            for b in range(TILES_PER_GATE):
+                quantise_tile(1 * TILES_PER_GATE + b, d_z_grouped[:, b])
+                multiply_rows(1 * TILES_PER_GATE + b)
+
+            r_slope(0)
+            times_h_n(0)
+            for b in range(TILES_PER_GATE):
+                if b + 1 < TILES_PER_GATE:
+                    r_slope(b + 1)
+                d_r_grouped = product_of(r_sb, d_n, b)
+                if b + 1 < TILES_PER_GATE:
+                    times_h_n(b + 1)
+                quantise_tile(b, d_r_grouped[:])
+                multiply_rows(b)

@@ -77,16 +77,16 @@ def tile_vrnncell_pc_v_kernel(
             tile, dram = streams[k // PASSES]
             load(tile, dram, k % PASSES)
 
-        def rows_side_by_side(dst, src):
-            nc.scalar.copy(
+        def rows_side_by_side(copy, dst, src):
+            copy(
                 out=dst.rearrange("p (c i) j -> p c j i", i=RUN),
                 in_=src.rearrange("p j (c i) -> p c j i", i=RUN),
             )
 
-        def regroup_chunk(k):
+        def regroup_chunk(k, copy):
             tile, dram = streams[k // PASSES]
             u_grouped[k] = group.tile([P, H, PACK], BF16, align_bytes=64, tag="wide", name="u_grouped")
-            rows_side_by_side(u_grouped[k][:], tile[:, k % PASSES])
+            rows_side_by_side(copy, u_grouped[k][:], tile[:, k % PASSES])
 
         def quantise_chunk(k):
             i, s = k // PASSES, k % PASSES
@@ -168,21 +168,30 @@ def tile_vrnncell_pc_v_kernel(
                     out=neg_ga[:, s], in0=zg_sb[:, s], scalar=1.0, in1=g_sb[:, s],
                     op0=ALU.subtract, op1=ALU.mult,
                 )
-                if s > 0:
-                    quantise_chunk(first - 1)
-                regroup_chunk(first)
+                regroup_chunk(first, nc.scalar.copy)
                 nc.vector.tensor_tensor(
                     out=zg_sb[:, s], in0=neg_ga[:, s], in1=zg_sb[:, s], op=ALU.mult
                 )
                 nc.scalar.activation(out=d_n[:, s], in_=n_sb[:, s], func=ACT.Square)
-                regroup_chunk(first + 1)
+                regroup_chunk(first + 1, nc.scalar.copy)
                 nc.vector.scalar_tensor_tensor(
                     out=d_n[:, s], in0=d_n[:, s], scalar=1.0, in1=neg_ga[:, s],
                     op0=ALU.subtract, op1=ALU.mult,
                 )
                 d_n_grouped = group.tile([P, H, PACK], BF16, align_bytes=64, tag="wide")
-                rows_side_by_side(d_n_grouped[:], d_n[:, s])
-                regroup_chunk(first + 2)
+                rows_side_by_side(nc.scalar.copy, d_n_grouped[:], d_n[:, s])
+                regroup_chunk(first + 2, nc.vector.tensor_copy)
+                quantise_chunk(first)
+                quantise_chunk(first + 1)
+                quantise_chunk(first + 2)
+                for b in range(TILES_PER_GATE):
+                    nc.vector.quantize_mx(
+                        out=dgi_codes[:, 2 * TILES_PER_GATE + b, s, :].bitcast(E5M2_X4),
+                        scales=dgi_scales[:, 2 * TILES_PER_GATE + b, s, :],
+                        in_=d_n_grouped[:, b * M_TILE : (b + 1) * M_TILE, :].rearrange(
+                            "p w j -> p (w j)"
+                        ),
+                    )
                 for b in range(TILES_PER_GATE):
                     cols = slice(b * M_TILE, (b + 1) * M_TILE)
                     n_minus_h = psum.tile([P, PACK, M_TILE], F32, tag="acc")
@@ -200,17 +209,6 @@ def tile_vrnncell_pc_v_kernel(
                         in1=zg_sb[:, s, :, cols].rearrange("p j w -> p w j"),
                         op=ALU.mult,
                     )
-                quantise_chunk(first)
-                quantise_chunk(first + 1)
-                for b in range(TILES_PER_GATE):
-                    nc.vector.quantize_mx(
-                        out=dgi_codes[:, 2 * TILES_PER_GATE + b, s, :].bitcast(E5M2_X4),
-                        scales=dgi_scales[:, 2 * TILES_PER_GATE + b, s, :],
-                        in_=d_n_grouped[:, b * M_TILE : (b + 1) * M_TILE, :].rearrange(
-                            "p w j -> p (w j)"
-                        ),
-                    )
-            quantise_chunk(PASSES * chunks_per_round - 1)
 
             for b in range(TILES_PER_GATE):
                 multiply_rows(2 * TILES_PER_GATE + b)

@@ -77,16 +77,16 @@ def tile_vrnncell_pc_v_kernel(
             tile, dram = streams[k // PASSES]
             load(tile, dram, k % PASSES)
 
-        def rows_side_by_side(copy, dst, src):
-            copy(
+        def rows_side_by_side(dst, src):
+            nc.scalar.copy(
                 out=dst.rearrange("p (c i) j -> p c j i", i=RUN),
                 in_=src.rearrange("p j (c i) -> p c j i", i=RUN),
             )
 
-        def regroup_chunk(k, copy):
+        def regroup_chunk(k):
             tile, dram = streams[k // PASSES]
             u_grouped[k] = group.tile([P, H, PACK], BF16, align_bytes=64, tag="wide", name="u_grouped")
-            rows_side_by_side(copy, u_grouped[k][:], tile[:, k % PASSES])
+            rows_side_by_side(u_grouped[k][:], tile[:, k % PASSES])
 
         def quantise_chunk(k):
             i, s = k // PASSES, k % PASSES
@@ -116,12 +116,13 @@ def tile_vrnncell_pc_v_kernel(
         def product_of(factor0, factor1, b):
             cols = slice(b * M_TILE, (b + 1) * M_TILE)
             grouped = group.tile([P, PASSES, M_TILE, PACK], BF16, align_bytes=64, tag="narrow")
-            nc.vector.tensor_tensor(
-                out=grouped[:],
-                in0=factor0[:, :, :, cols].rearrange("p s j w -> p s w j"),
-                in1=factor1[:, :, :, cols].rearrange("p s j w -> p s w j"),
-                op=ALU.mult,
-            )
+            for s in range(PASSES):
+                nc.vector.tensor_tensor(
+                    out=grouped[:, s].rearrange("p (c i) j -> p c j i", i=RUN),
+                    in0=factor0[:, s, :, cols].rearrange("p j (c i) -> p c j i", i=RUN),
+                    in1=factor1[:, s, :, cols].rearrange("p j (c i) -> p c j i", i=RUN),
+                    op=ALU.mult,
+                )
             return grouped
 
         def quantise_tile(m, grouped):
@@ -168,30 +169,21 @@ def tile_vrnncell_pc_v_kernel(
                     out=neg_ga[:, s], in0=zg_sb[:, s], scalar=1.0, in1=g_sb[:, s],
                     op0=ALU.subtract, op1=ALU.mult,
                 )
-                regroup_chunk(first, nc.scalar.copy)
+                if s > 0:
+                    quantise_chunk(first - 1)
+                regroup_chunk(first)
                 nc.vector.tensor_tensor(
                     out=zg_sb[:, s], in0=neg_ga[:, s], in1=zg_sb[:, s], op=ALU.mult
                 )
                 nc.scalar.activation(out=d_n[:, s], in_=n_sb[:, s], func=ACT.Square)
-                regroup_chunk(first + 1, nc.scalar.copy)
+                regroup_chunk(first + 1)
                 nc.vector.scalar_tensor_tensor(
                     out=d_n[:, s], in0=d_n[:, s], scalar=1.0, in1=neg_ga[:, s],
                     op0=ALU.subtract, op1=ALU.mult,
                 )
                 d_n_grouped = group.tile([P, H, PACK], BF16, align_bytes=64, tag="wide")
-                rows_side_by_side(nc.scalar.copy, d_n_grouped[:], d_n[:, s])
-                regroup_chunk(first + 2, nc.vector.tensor_copy)
-                quantise_chunk(first)
-                quantise_chunk(first + 1)
-                quantise_chunk(first + 2)
-                for b in range(TILES_PER_GATE):
-                    nc.vector.quantize_mx(
-                        out=dgi_codes[:, 2 * TILES_PER_GATE + b, s, :].bitcast(E5M2_X4),
-                        scales=dgi_scales[:, 2 * TILES_PER_GATE + b, s, :],
-                        in_=d_n_grouped[:, b * M_TILE : (b + 1) * M_TILE, :].rearrange(
-                            "p w j -> p (w j)"
-                        ),
-                    )
+                rows_side_by_side(d_n_grouped[:], d_n[:, s])
+                regroup_chunk(first + 2)
                 for b in range(TILES_PER_GATE):
                     cols = slice(b * M_TILE, (b + 1) * M_TILE)
                     n_minus_h = psum.tile([P, PACK, M_TILE], F32, tag="acc")
@@ -204,11 +196,22 @@ def tile_vrnncell_pc_v_kernel(
                         start=False, stop=True,
                     )
                     nc.vector.tensor_tensor(
-                        out=d_z_grouped[:, b, s],
-                        in0=n_minus_h[:].rearrange("p j w -> p w j"),
-                        in1=zg_sb[:, s, :, cols].rearrange("p j w -> p w j"),
+                        out=d_z_grouped[:, b, s].rearrange("p (c i) j -> p c j i", i=RUN),
+                        in0=n_minus_h[:].rearrange("p j (c i) -> p c j i", i=RUN),
+                        in1=zg_sb[:, s, :, cols].rearrange("p j (c i) -> p c j i", i=RUN),
                         op=ALU.mult,
                     )
+                quantise_chunk(first)
+                quantise_chunk(first + 1)
+                for b in range(TILES_PER_GATE):
+                    nc.vector.quantize_mx(
+                        out=dgi_codes[:, 2 * TILES_PER_GATE + b, s, :].bitcast(E5M2_X4),
+                        scales=dgi_scales[:, 2 * TILES_PER_GATE + b, s, :],
+                        in_=d_n_grouped[:, b * M_TILE : (b + 1) * M_TILE, :].rearrange(
+                            "p w j -> p (w j)"
+                        ),
+                    )
+            quantise_chunk(PASSES * chunks_per_round - 1)
 
             for b in range(TILES_PER_GATE):
                 multiply_rows(2 * TILES_PER_GATE + b)

@@ -23,6 +23,7 @@ STREAMS = 3
 M_TILE = 128
 TILES_PER_GATE = H // M_TILE
 RUN = 4
+R_GATE, Z_GATE, N_GATE = 0, 1, 2
 
 FLOPS = 2 * TOKENS * (GATES * H) * (STREAMS * H)
 BYTES = 2 * 5 * TOKENS * H + 4 * (GATES + 1) * TOKENS * H + 4 * (GATES * H) * (STREAMS * H)
@@ -32,13 +33,22 @@ def tokens_by_pass(dram):
     return dram.rearrange("(s p j) w -> s p j w", s=PASSES, p=P, j=PACK)
 
 
+def by_runs_out(grouped):
+    return grouped.rearrange("p (c i) j -> p c j i", i=RUN)
+
+
+def by_runs_in(rows):
+    return rows.rearrange("p j (c i) -> p c j i", i=RUN)
+
+
 def tile_vrnncell_pc_v_kernel(
     tc, x_t, z_t, a_prev, h_prev, w_ih, w_hh, b_ih, b_hh, gates, h_n, grad_out, out
 ):
     nc = tc.nc
     with ExitStack() as ctx:
         keep = ctx.enter_context(tc.tile_pool(name="keep", bufs=1))
-        group = ctx.enter_context(tc.tile_pool(name="group", bufs=4))
+        wide = ctx.enter_context(tc.tile_pool(name="wide", bufs=5))
+        narrow = ctx.enter_context(tc.tile_pool(name="narrow", bufs=3))
         stage = ctx.enter_context(tc.tile_pool(name="stage", bufs=5))
         psum = ctx.enter_context(tc.psum_pool(name="psum", bufs=8))
 
@@ -54,12 +64,14 @@ def tile_vrnncell_pc_v_kernel(
         hn_sb = keep.tile(whole, F32)
         neg_ga = keep.tile(whole, F32)
         d_n = keep.tile(whole, F32)
-        d_z_grouped = keep.tile([P, TILES_PER_GATE, PASSES, M_TILE, PACK], BF16, align_bytes=64)
+        d_z_grouped = keep.tile([P, PASSES, H, PACK], BF16, align_bytes=64)
         ident = keep.tile([P, P], F32)
         neg_ident = keep.tile([P, P], BF16)
 
-        dgi_codes = keep.tile([P, GATES * TILES_PER_GATE, PASSES, M_TILE], U32, align_bytes=64)
-        dgi_scales = keep.tile([P, GATES * TILES_PER_GATE, PASSES, M_TILE], U8, align_bytes=64)
+        nz_codes = keep.tile([P, 2, PASSES, H], U32, align_bytes=64)
+        nz_scales = keep.tile([P, 2, PASSES, H], U8, align_bytes=64)
+        r_codes = keep.tile([P, TILES_PER_GATE, PASSES, M_TILE], U32, align_bytes=64)
+        r_scales = keep.tile([P, TILES_PER_GATE, PASSES, M_TILE], U8, align_bytes=64)
         u_codes = keep.tile([P, PASSES, STREAMS * H], U32, align_bytes=64)
         u_scales = keep.tile([P, PASSES, STREAMS * H], U8, align_bytes=64)
 
@@ -70,162 +82,243 @@ def tile_vrnncell_pc_v_kernel(
         zg_dram = gates[:, 1 * H : 2 * H]
         n_dram = gates[:, 2 * H : 3 * H]
         streams = [(x_sb, x_t), (z_sb, z_t), (a_sb, a_prev)]
-        chunks_per_round = STREAMS
+        X, Z, A = 0, 1, 2
         u_grouped = {}
+        dn_grouped = {}
+        n_minus_h = {}
+        acc = {}
+        rows = {}
 
-        def load_chunk(k):
-            tile, dram = streams[k // PASSES]
-            load(tile, dram, k % PASSES)
+        def copy_on(engine, dst, src):
+            if engine == "S":
+                nc.scalar.copy(out=dst, in_=src)
+            else:
+                nc.vector.tensor_copy(out=dst, in_=src)
 
-        def rows_side_by_side(dst, src):
-            nc.scalar.copy(
-                out=dst.rearrange("p (c i) j -> p c j i", i=RUN),
-                in_=src.rearrange("p j (c i) -> p c j i", i=RUN),
-            )
+        def load_u(i, s):
+            tile, dram = streams[i]
+            load(tile, dram, s)
 
-        def regroup_chunk(k):
-            tile, dram = streams[k // PASSES]
-            u_grouped[k] = group.tile([P, H, PACK], BF16, align_bytes=64, tag="wide", name="u_grouped")
-            rows_side_by_side(u_grouped[k][:], tile[:, k % PASSES])
+        def regroup_u(engine, i, s):
+            grouped = wide.tile([P, H, PACK], BF16, align_bytes=64, tag="wide", name="u_grouped")
+            u_grouped[(i, s)] = grouped
+            copy_on(engine, by_runs_out(grouped[:]), by_runs_in(streams[i][0][:, s]))
 
-        def quantise_chunk(k):
-            i, s = k // PASSES, k % PASSES
+        def quantise_u(i, s):
             nc.vector.quantize_mx(
                 out=u_codes[:, s, i * H : (i + 1) * H].bitcast(E4M3_X4),
                 scales=u_scales[:, s, i * H : (i + 1) * H],
-                in_=u_grouped[k][:].rearrange("p w j -> p (w j)"),
+                in_=u_grouped[(i, s)][:].rearrange("p w j -> p (w j)"),
             )
 
-        def multiply_rows(m):
-            rows = stage.tile([P, STREAMS * H], F32)
-            for i in range(STREAMS):
-                acc = psum.tile([P, H], F32, tag="acc")
-                for s in range(PASSES):
-                    nc.tensor.matmul_mx(
-                        out=acc[:],
-                        lhsT=dgi_codes[:, m, s, :].bitcast(E5M2_X4),
-                        lhsT_scale=dgi_scales[:, m, s, :],
-                        rhs=u_codes[:, s, i * H : (i + 1) * H].bitcast(E4M3_X4),
-                        rhs_scale=u_scales[:, s, i * H : (i + 1) * H],
-                        start=(s == 0),
-                        stop=(s == PASSES - 1),
-                    )
-                nc.scalar.copy(out=rows[:, i * H : (i + 1) * H], in_=acc[:])
-            nc.sync.dma_start(out=out[m * M_TILE : (m + 1) * M_TILE, :], in_=rows[:])
-
-        def product_of(factor0, factor1, b):
-            cols = slice(b * M_TILE, (b + 1) * M_TILE)
-            grouped = group.tile([P, PASSES, M_TILE, PACK], BF16, align_bytes=64, tag="narrow")
-            for s in range(PASSES):
-                nc.vector.tensor_tensor(
-                    out=grouped[:, s].rearrange("p (c i) j -> p c j i", i=RUN),
-                    in0=factor0[:, s, :, cols].rearrange("p j (c i) -> p c j i", i=RUN),
-                    in1=factor1[:, s, :, cols].rearrange("p j (c i) -> p c j i", i=RUN),
-                    op=ALU.mult,
-                )
-            return grouped
-
-        def quantise_tile(m, grouped):
-            nc.vector.quantize_mx(
-                out=dgi_codes[:, m].rearrange("p s w -> p (s w)").bitcast(E5M2_X4),
-                scales=dgi_scales[:, m].rearrange("p s w -> p (s w)"),
-                in_=grouped.rearrange("p s w j -> p (s w j)"),
-            )
-
-        def r_slope(b):
-            cols = slice(b * M_TILE, (b + 1) * M_TILE)
+        def make_neg_ga(s):
             nc.vector.scalar_tensor_tensor(
-                out=r_sb[:, :, :, cols], in0=r_sb[:, :, :, cols], scalar=1.0,
-                in1=r_sb[:, :, :, cols], op0=ALU.subtract, op1=ALU.mult,
+                out=neg_ga[:, s], in0=zg_sb[:, s], scalar=1.0, in1=g_sb[:, s],
+                op0=ALU.subtract, op1=ALU.mult,
             )
+
+        def make_z_factor(s):
+            nc.vector.tensor_tensor(out=zg_sb[:, s], in0=neg_ga[:, s], in1=zg_sb[:, s], op=ALU.mult)
+
+        def square_n(s):
+            nc.scalar.activation(out=d_n[:, s], in_=n_sb[:, s], func=ACT.Square)
+
+        def make_d_n(s):
+            nc.vector.scalar_tensor_tensor(
+                out=d_n[:, s], in0=d_n[:, s], scalar=1.0, in1=neg_ga[:, s],
+                op0=ALU.subtract, op1=ALU.mult,
+            )
+
+        def regroup_d_n(engine, s):
+            grouped = wide.tile([P, H, PACK], BF16, align_bytes=64, tag="wide", name="dn_grouped")
+            dn_grouped[s] = grouped
+            copy_on(engine, by_runs_out(grouped[:]), by_runs_in(d_n[:, s]))
+
+        def quantise_pass(which, s, grouped):
+            nc.vector.quantize_mx(
+                out=nz_codes[:, which, s, :].bitcast(E5M2_X4),
+                scales=nz_scales[:, which, s, :],
+                in_=grouped.rearrange("p w j -> p (w j)"),
+            )
+
+        def subtract_h(s, b):
+            cols = slice(b * M_TILE, (b + 1) * M_TILE)
+            bank = psum.tile([P, PACK, M_TILE], F32, tag="acc", name="n_minus_h")
+            n_minus_h[(s, b)] = bank
+            nc.tensor.matmul(out=bank[:], lhsT=ident[:], rhs=n_sb[:, s, :, cols], start=True, stop=False)
+            nc.tensor.matmul(out=bank[:], lhsT=neg_ident[:], rhs=h_sb[:, s, :, cols], start=False, stop=True)
+
+        def make_d_z(s, b):
+            cols = slice(b * M_TILE, (b + 1) * M_TILE)
+            nc.vector.tensor_tensor(
+                out=by_runs_out(d_z_grouped[:, s, cols, :]),
+                in0=by_runs_in(n_minus_h[(s, b)][:]),
+                in1=by_runs_in(zg_sb[:, s, :, cols]),
+                op=ALU.mult,
+            )
+
+        def square_r(s):
+            nc.scalar.activation(out=r_sb[:, s], in_=r_sb[:, s], func=ACT.Square, bias=-0.5, scale=1.0)
 
         def times_h_n(b):
             cols = slice(b * M_TILE, (b + 1) * M_TILE)
             nc.vector.scalar_tensor_tensor(
-                out=r_sb[:, :, :, cols], in0=r_sb[:, :, :, cols], scalar=-1.0,
-                in1=hn_sb[:, :, :, cols], op0=ALU.mult, op1=ALU.mult,
+                out=r_sb[:, :, :, cols], in0=r_sb[:, :, :, cols], scalar=0.25,
+                in1=hn_sb[:, :, :, cols], op0=ALU.subtract, op1=ALU.mult,
             )
+
+        dr_grouped = {}
+
+        def make_d_r(b):
+            cols = slice(b * M_TILE, (b + 1) * M_TILE)
+            grouped = narrow.tile([P, PASSES, M_TILE, PACK], BF16, align_bytes=64, tag="narrow", name="dr_grouped")
+            dr_grouped[b] = grouped
+            for s in range(PASSES):
+                nc.vector.scalar_tensor_tensor(
+                    out=grouped[:, s],
+                    in0=r_sb[:, s, :, cols].rearrange("p j w -> p w j"), scalar=-1.0,
+                    in1=d_n[:, s, :, cols].rearrange("p j w -> p w j"),
+                    op0=ALU.mult, op1=ALU.mult,
+                )
+
+        def quantise_d_r(b):
+            nc.vector.quantize_mx(
+                out=r_codes[:, b].rearrange("p s w -> p (s w)").bitcast(E5M2_X4),
+                scales=r_scales[:, b].rearrange("p s w -> p (s w)"),
+                in_=dr_grouped[b][:].rearrange("p s w j -> p (s w j)"),
+            )
+
+        def stationary(gate, b, s):
+            cols = slice(b * M_TILE, (b + 1) * M_TILE)
+            if gate == R_GATE:
+                return r_codes[:, b, s, :], r_scales[:, b, s, :]
+            which = 0 if gate == N_GATE else 1
+            return nz_codes[:, which, s, cols], nz_scales[:, which, s, cols]
+
+        def multiply(gate, b, i):
+            bank = psum.tile([P, H], F32, tag="acc", name="acc")
+            acc[(gate, b, i)] = bank
+            for s in range(PASSES):
+                codes, scales = stationary(gate, b, s)
+                nc.tensor.matmul_mx(
+                    out=bank[:],
+                    lhsT=codes.bitcast(E5M2_X4),
+                    lhsT_scale=scales,
+                    rhs=u_codes[:, s, i * H : (i + 1) * H].bitcast(E4M3_X4),
+                    rhs_scale=u_scales[:, s, i * H : (i + 1) * H],
+                    start=(s == 0),
+                    stop=(s == PASSES - 1),
+                )
+
+        def empty(engine, gate, b, i):
+            if (gate, b) not in rows:
+                rows[(gate, b)] = stage.tile([P, STREAMS * H], F32, tag="rows", name="rows")
+            copy_on(engine, rows[(gate, b)][:, i * H : (i + 1) * H], acc[(gate, b, i)][:])
+
+        def store(gate, b):
+            m = gate * TILES_PER_GATE + b
+            nc.sync.dma_start(out=out[m * M_TILE : (m + 1) * M_TILE, :], in_=rows[(gate, b)][:])
+
+        def row_tile(gate, b, engines):
+            for i in range(STREAMS):
+                multiply(gate, b, i)
+            for i in range(STREAMS):
+                empty(engines[i], gate, b, i)
+            store(gate, b)
 
         with tc.manual_schedule():
             make_identity(nc, ident[:])
             nc.scalar.mul(out=neg_ident[:], in_=ident[:], mul=-1.0)
-            for s in range(PASSES):
-                first = s * chunks_per_round
-                load(g_sb, grad_out, s)
-                load(zg_sb, zg_dram, s)
-                load_chunk(first)
-                load(n_sb, n_dram, s)
-                load(h_sb, h_prev, s)
-                load_chunk(first + 1)
-                load_chunk(first + 2)
-            for s in range(PASSES):
-                load(r_sb, r_dram, s)
-            for s in range(PASSES):
-                load(hn_sb, h_n, s)
 
-            for s in range(PASSES):
-                first = s * chunks_per_round
-                nc.vector.scalar_tensor_tensor(
-                    out=neg_ga[:, s], in0=zg_sb[:, s], scalar=1.0, in1=g_sb[:, s],
-                    op0=ALU.subtract, op1=ALU.mult,
-                )
-                if s > 0:
-                    quantise_chunk(first - 1)
-                regroup_chunk(first)
-                nc.vector.tensor_tensor(
-                    out=zg_sb[:, s], in0=neg_ga[:, s], in1=zg_sb[:, s], op=ALU.mult
-                )
-                nc.scalar.activation(out=d_n[:, s], in_=n_sb[:, s], func=ACT.Square)
-                regroup_chunk(first + 1)
-                nc.vector.scalar_tensor_tensor(
-                    out=d_n[:, s], in0=d_n[:, s], scalar=1.0, in1=neg_ga[:, s],
-                    op0=ALU.subtract, op1=ALU.mult,
-                )
-                d_n_grouped = group.tile([P, H, PACK], BF16, align_bytes=64, tag="wide")
-                rows_side_by_side(d_n_grouped[:], d_n[:, s])
-                regroup_chunk(first + 2)
-                for b in range(TILES_PER_GATE):
-                    cols = slice(b * M_TILE, (b + 1) * M_TILE)
-                    n_minus_h = psum.tile([P, PACK, M_TILE], F32, tag="acc")
-                    nc.tensor.matmul(
-                        out=n_minus_h[:], lhsT=ident[:], rhs=n_sb[:, s, :, cols],
-                        start=True, stop=False,
-                    )
-                    nc.tensor.matmul(
-                        out=n_minus_h[:], lhsT=neg_ident[:], rhs=h_sb[:, s, :, cols],
-                        start=False, stop=True,
-                    )
-                    nc.vector.tensor_tensor(
-                        out=d_z_grouped[:, b, s].rearrange("p (c i) j -> p c j i", i=RUN),
-                        in0=n_minus_h[:].rearrange("p j (c i) -> p c j i", i=RUN),
-                        in1=zg_sb[:, s, :, cols].rearrange("p j (c i) -> p c j i", i=RUN),
-                        op=ALU.mult,
-                    )
-                quantise_chunk(first)
-                quantise_chunk(first + 1)
-                for b in range(TILES_PER_GATE):
-                    nc.vector.quantize_mx(
-                        out=dgi_codes[:, 2 * TILES_PER_GATE + b, s, :].bitcast(E5M2_X4),
-                        scales=dgi_scales[:, 2 * TILES_PER_GATE + b, s, :],
-                        in_=d_n_grouped[:, b * M_TILE : (b + 1) * M_TILE, :].rearrange(
-                            "p w j -> p (w j)"
-                        ),
-                    )
-            quantise_chunk(PASSES * chunks_per_round - 1)
+            load_u(X, 0)
+            load_u(X, 1)
+            load_u(Z, 0)
+            load(g_sb, grad_out, 0)
+            load(zg_sb, zg_dram, 0)
+            load(n_sb, n_dram, 0)
+            load(h_sb, h_prev, 0)
+            load_u(Z, 1)
+            load(g_sb, grad_out, 1)
+            load(zg_sb, zg_dram, 1)
+            load(n_sb, n_dram, 1)
+            load(h_sb, h_prev, 1)
+            load_u(A, 0)
+            load_u(A, 1)
+            load(r_sb, r_dram, 0)
+            load(r_sb, r_dram, 1)
+            load(hn_sb, h_n, 0)
+            load(hn_sb, h_n, 1)
 
+            regroup_u("V", X, 0)
+            regroup_u("S", X, 1)
+            quantise_u(X, 0)
+            regroup_u("V", Z, 0)
+            quantise_u(X, 1)
+            quantise_u(Z, 0)
+            make_neg_ga(0)
+            square_n(0)
+            make_z_factor(0)
             for b in range(TILES_PER_GATE):
-                multiply_rows(2 * TILES_PER_GATE + b)
+                subtract_h(0, b)
+            regroup_u("S", Z, 1)
+            make_d_n(0)
+            regroup_d_n("S", 0)
+            make_d_z(0, 0)
+            quantise_u(Z, 1)
+            make_neg_ga(1)
+            square_n(1)
+            quantise_pass(0, 0, dn_grouped[0][:])
+            make_z_factor(1)
             for b in range(TILES_PER_GATE):
-                quantise_tile(1 * TILES_PER_GATE + b, d_z_grouped[:, b])
-                multiply_rows(1 * TILES_PER_GATE + b)
+                subtract_h(1, b)
+            regroup_u("S", A, 0)
+            make_d_n(1)
+            regroup_u("S", A, 1)
+            quantise_u(A, 0)
+            regroup_d_n("V", 1)
+            quantise_u(A, 1)
+            quantise_pass(0, 1, dn_grouped[1][:])
+            square_r(0)
 
-            r_slope(0)
+            make_d_z(0, 1)
+            make_d_z(0, 2)
+            for i in range(STREAMS):
+                multiply(N_GATE, 0, i)
+            make_d_z(0, 3)
+            make_d_z(1, 0)
+            make_d_z(1, 1)
+            for i in range(STREAMS):
+                empty("S", N_GATE, 0, i)
+            store(N_GATE, 0)
+            for i in range(STREAMS):
+                multiply(N_GATE, 1, i)
+            make_d_z(1, 2)
+            make_d_z(1, 3)
+            for i in range(STREAMS):
+                empty("SSV"[i], N_GATE, 1, i)
+            store(N_GATE, 1)
+            square_r(1)
+            quantise_pass(1, 0, d_z_grouped[:, 0])
+            quantise_pass(1, 1, d_z_grouped[:, 1])
+            row_tile(N_GATE, 2, "VVS")
+            row_tile(N_GATE, 3, "VSS")
             times_h_n(0)
-            for b in range(TILES_PER_GATE):
-                if b + 1 < TILES_PER_GATE:
-                    r_slope(b + 1)
-                d_r_grouped = product_of(r_sb, d_n, b)
-                if b + 1 < TILES_PER_GATE:
-                    times_h_n(b + 1)
-                quantise_tile(b, d_r_grouped[:])
-                multiply_rows(b)
+            times_h_n(1)
+            row_tile(Z_GATE, 0, "SSS")
+            make_d_r(0)
+            make_d_r(1)
+            quantise_d_r(0)
+            row_tile(Z_GATE, 1, "SSS")
+            times_h_n(2)
+            quantise_d_r(1)
+            row_tile(Z_GATE, 2, "SSS")
+            make_d_r(2)
+            times_h_n(3)
+            quantise_d_r(2)
+            row_tile(Z_GATE, 3, "SSS")
+            row_tile(R_GATE, 0, "SSS")
+            make_d_r(3)
+            quantise_d_r(3)
+            row_tile(R_GATE, 1, "SSS")
+            row_tile(R_GATE, 2, "SSV")
+            row_tile(R_GATE, 3, "SVS")

@@ -219,6 +219,17 @@ def tile_vrnncell_pc_v_kernel(
             m = gate * TILES_PER_GATE + b
             nc.sync.dma_start(out=out[m * M_TILE : (m + 1) * M_TILE, :], in_=rows[(gate, b)][:])
 
+        def last_row_tile(gate, b, engines):
+            m = gate * TILES_PER_GATE + b
+            for i in range(STREAMS):
+                multiply(gate, b, i)
+            for i in range(STREAMS):
+                empty(engines[i], gate, b, i)
+                nc.sync.dma_start(
+                    out=out[m * M_TILE : (m + 1) * M_TILE, i * H : (i + 1) * H],
+                    in_=rows[(gate, b)][:, i * H : (i + 1) * H],
+                )
+
         def row_tile(gate, b, engines):
             for i in range(STREAMS):
                 multiply(gate, b, i)
@@ -321,4 +332,4 @@ def tile_vrnncell_pc_v_kernel(
             quantise_d_r(3)
             row_tile(R_GATE, 1, "SSS")
             row_tile(R_GATE, 2, "SSV")
-            row_tile(R_GATE, 3, "SVS")
+            last_row_tile(R_GATE, 3, "SVS")

@@ -59,8 +59,7 @@ def tile_vrnncell_pc_v_kernel(
         z_sb = keep.tile(whole, BF16)
         a_sb = keep.tile(whole, BF16)
         r_sb = keep.tile(whole, F32)
-        zg_sb = keep.tile(whole, F32)
-        n_sb = keep.tile(whole, F32)
+        zn_sb = keep.tile([P, PASSES, PACK, 2 * H], F32)
         hn_sb = keep.tile(whole, F32)
         neg_ga = keep.tile(whole, F32)
         d_n = keep.tile(whole, F32)
@@ -79,8 +78,8 @@ def tile_vrnncell_pc_v_kernel(
             nc.sync.dma_start(out=tile[:, s], in_=tokens_by_pass(dram)[s])
 
         r_dram = gates[:, 0 * H : 1 * H]
-        zg_dram = gates[:, 1 * H : 2 * H]
-        n_dram = gates[:, 2 * H : 3 * H]
+        zn_dram = gates[:, 1 * H : 3 * H]
+        HALF = PACK // 2
         streams = [(x_sb, x_t), (z_sb, z_t), (a_sb, a_prev)]
         X, Z, A = 0, 1, 2
         u_grouped = {}
@@ -111,17 +110,26 @@ def tile_vrnncell_pc_v_kernel(
                 in_=u_grouped[(i, s)][:].rearrange("p w j -> p (w j)"),
             )
 
-        def make_neg_ga(s):
+        def load_zn(s, half):
+            js = slice(half * HALF, (half + 1) * HALF)
+            nc.sync.dma_start(out=zn_sb[:, s, js, :], in_=tokens_by_pass(zn_dram)[s][:, js, :])
+
+        def make_neg_ga(s, half):
+            js = slice(half * HALF, (half + 1) * HALF)
             nc.vector.scalar_tensor_tensor(
-                out=neg_ga[:, s], in0=zg_sb[:, s], scalar=1.0, in1=g_sb[:, s],
+                out=neg_ga[:, s, js], in0=zn_sb[:, s, js, 0:H], scalar=1.0, in1=g_sb[:, s, js],
                 op0=ALU.subtract, op1=ALU.mult,
             )
 
-        def make_z_factor(s):
-            nc.vector.tensor_tensor(out=zg_sb[:, s], in0=neg_ga[:, s], in1=zg_sb[:, s], op=ALU.mult)
+        def make_z_factor(s, half):
+            js = slice(half * HALF, (half + 1) * HALF)
+            nc.vector.tensor_tensor(
+                out=zn_sb[:, s, js, 0:H], in0=neg_ga[:, s, js], in1=zn_sb[:, s, js, 0:H], op=ALU.mult
+            )
 
-        def square_n(s):
-            nc.scalar.activation(out=d_n[:, s], in_=n_sb[:, s], func=ACT.Square)
+        def square_n(s, half):
+            js = slice(half * HALF, (half + 1) * HALF)
+            nc.scalar.activation(out=d_n[:, s, js], in_=zn_sb[:, s, js, H : 2 * H], func=ACT.Square)
 
         def make_d_n(s):
             nc.vector.scalar_tensor_tensor(
@@ -145,7 +153,8 @@ def tile_vrnncell_pc_v_kernel(
             cols = slice(b * M_TILE, (b + 1) * M_TILE)
             bank = psum.tile([P, PACK, M_TILE], F32, tag="acc", name="n_minus_h")
             n_minus_h[(s, b)] = bank
-            nc.tensor.matmul(out=bank[:], lhsT=ident[:], rhs=n_sb[:, s, :, cols], start=True, stop=False)
+            n_cols = slice(H + b * M_TILE, H + (b + 1) * M_TILE)
+            nc.tensor.matmul(out=bank[:], lhsT=ident[:], rhs=zn_sb[:, s, :, n_cols], start=True, stop=False)
             nc.tensor.matmul(out=bank[:], lhsT=neg_ident[:], rhs=h_sb[:, s, :, cols], start=False, stop=True)
 
         def make_d_z(s, b):
@@ -153,7 +162,7 @@ def tile_vrnncell_pc_v_kernel(
             nc.vector.tensor_tensor(
                 out=by_runs_out(d_z_grouped[:, s, cols, :]),
                 in0=by_runs_in(n_minus_h[(s, b)][:]),
-                in1=by_runs_in(zg_sb[:, s, :, cols]),
+                in1=by_runs_in(zn_sb[:, s, :, cols]),
                 op=ALU.mult,
             )
 
@@ -245,13 +254,13 @@ def tile_vrnncell_pc_v_kernel(
             load_u(X, 1)
             load_u(Z, 0)
             load(g_sb, grad_out, 0)
-            load(zg_sb, zg_dram, 0)
-            load(n_sb, n_dram, 0)
+            load_zn(0, 0)
+            load_zn(0, 1)
             load(h_sb, h_prev, 0)
             load_u(Z, 1)
             load(g_sb, grad_out, 1)
-            load(zg_sb, zg_dram, 1)
-            load(n_sb, n_dram, 1)
+            load_zn(1, 0)
+            load_zn(1, 1)
             load(h_sb, h_prev, 1)
             load_u(A, 0)
             load_u(A, 1)
@@ -266,9 +275,10 @@ def tile_vrnncell_pc_v_kernel(
             regroup_u("V", Z, 0)
             quantise_u(X, 1)
             quantise_u(Z, 0)
-            make_neg_ga(0)
-            square_n(0)
-            make_z_factor(0)
+            for half in range(2):
+                make_neg_ga(0, half)
+                square_n(0, half)
+                make_z_factor(0, half)
             for b in range(TILES_PER_GATE):
                 subtract_h(0, b)
             regroup_u("S", Z, 1)
@@ -276,10 +286,13 @@ def tile_vrnncell_pc_v_kernel(
             regroup_d_n("S", 0)
             make_d_z(0, 0)
             quantise_u(Z, 1)
-            make_neg_ga(1)
-            square_n(1)
+            make_neg_ga(1, 0)
+            square_n(1, 0)
             quantise_pass(0, 0, dn_grouped[0][:])
-            make_z_factor(1)
+            make_z_factor(1, 0)
+            make_neg_ga(1, 1)
+            square_n(1, 1)
+            make_z_factor(1, 1)
             for b in range(TILES_PER_GATE):
                 subtract_h(1, b)
             regroup_u("S", A, 0)

@@ -319,13 +319,13 @@ def tile_vrnncell_pc_v_kernel(
             make_d_z(1, 2)
             make_d_z(1, 3)
             for i in range(STREAMS):
-                empty("SSV"[i], N_GATE, 1, i)
+                empty("S", N_GATE, 1, i)
             store(N_GATE, 1)
-            square_r(1)
             quantise_pass(1, 0, d_z_grouped[:, 0])
             quantise_pass(1, 1, d_z_grouped[:, 1])
-            row_tile(N_GATE, 2, "VVS")
-            row_tile(N_GATE, 3, "VSS")
+            row_tile(N_GATE, 2, "SSV")
+            row_tile(N_GATE, 3, "VVV")
+            square_r(1)
             times_h_n(0)
             times_h_n(1)
             row_tile(Z_GATE, 0, "SSS")

from contextlib import ExitStack

import concourse.mybir as mybir
from concourse.masks import make_identity

F32 = mybir.dt.float32
BF16 = mybir.dt.bfloat16
U32 = mybir.dt.uint32
U8 = mybir.dt.uint8
E4M3_X4 = mybir.dt.float8_e4m3fn_x4
E5M2_X4 = mybir.dt.float8_e5m2_x4
ALU = mybir.AluOpType
ACT = mybir.ActivationFunctionType

P = 128
PACK = 4
K_PASS = P * PACK
TOKENS = 1024
PASSES = TOKENS // K_PASS
H = 512
GATES = 3
STREAMS = 3
M_TILE = 128
TILES_PER_GATE = H // M_TILE
RUN = 4
R_GATE, Z_GATE, N_GATE = 0, 1, 2

FLOPS = 2 * TOKENS * (GATES * H) * (STREAMS * H)
BYTES = 2 * 5 * TOKENS * H + 4 * (GATES + 1) * TOKENS * H + 4 * (GATES * H) * (STREAMS * H)


def tokens_by_pass(dram):
    return dram.rearrange("(s p j) w -> s p j w", s=PASSES, p=P, j=PACK)


def by_runs_out(grouped):
    return grouped.rearrange("p (c i) j -> p c j i", i=RUN)


def by_runs_in(rows):
    return rows.rearrange("p j (c i) -> p c j i", i=RUN)


def tile_vrnncell_pc_v_kernel(
    tc, x_t, z_t, a_prev, h_prev, w_ih, w_hh, b_ih, b_hh, gates, h_n, grad_out, out
):
    nc = tc.nc
    with ExitStack() as ctx:
        keep = ctx.enter_context(tc.tile_pool(name="keep", bufs=1))
        wide = ctx.enter_context(tc.tile_pool(name="wide", bufs=5))
        narrow = ctx.enter_context(tc.tile_pool(name="narrow", bufs=3))
        stage = ctx.enter_context(tc.tile_pool(name="stage", bufs=5))
        psum = ctx.enter_context(tc.psum_pool(name="psum", bufs=8))

        whole = [P, PASSES, PACK, H]
        g_sb = keep.tile(whole, BF16)
        h_sb = keep.tile(whole, BF16)
        x_sb = keep.tile(whole, BF16)
        z_sb = keep.tile(whole, BF16)
        a_sb = keep.tile(whole, BF16)
        r_sb = keep.tile(whole, F32)
        zn_sb = keep.tile([P, PASSES, PACK, 2 * H], F32)
        hn_sb = keep.tile(whole, F32)
        neg_ga = keep.tile(whole, F32)
        d_n = keep.tile(whole, F32)
        d_z_grouped = keep.tile([P, PASSES, H, PACK], BF16, align_bytes=64)
        ident = keep.tile([P, P], F32)
        neg_ident = keep.tile([P, P], BF16)

        nz_codes = keep.tile([P, 2, PASSES, H], U32, align_bytes=64)
        nz_scales = keep.tile([P, 2, PASSES, H], U8, align_bytes=64)
        r_codes = keep.tile([P, TILES_PER_GATE, PASSES, M_TILE], U32, align_bytes=64)
        r_scales = keep.tile([P, TILES_PER_GATE, PASSES, M_TILE], U8, align_bytes=64)
        u_codes = keep.tile([P, PASSES, STREAMS * H], U32, align_bytes=64)
        u_scales = keep.tile([P, PASSES, STREAMS * H], U8, align_bytes=64)

        def load(tile, dram, s):
            nc.sync.dma_start(out=tile[:, s], in_=tokens_by_pass(dram)[s])

        r_dram = gates[:, 0 * H : 1 * H]
        zn_dram = gates[:, 1 * H : 3 * H]
        HALF = PACK // 2
        streams = [(x_sb, x_t), (z_sb, z_t), (a_sb, a_prev)]
        X, Z, A = 0, 1, 2
        u_grouped = {}
        dn_grouped = {}
        n_minus_h = {}
        acc = {}
        rows = {}

        def copy_on(engine, dst, src):
            if engine == "S":
                nc.scalar.copy(out=dst, in_=src)
            else:
                nc.vector.tensor_copy(out=dst, in_=src)

        def load_u(i, s):
            tile, dram = streams[i]
            load(tile, dram, s)

        def regroup_u(engine, i, s):
            grouped = wide.tile([P, H, PACK], BF16, align_bytes=64, tag="wide", name="u_grouped")
            u_grouped[(i, s)] = grouped
            copy_on(engine, by_runs_out(grouped[:]), by_runs_in(streams[i][0][:, s]))

        def quantise_u(i, s):
            nc.vector.quantize_mx(
                out=u_codes[:, s, i * H : (i + 1) * H].bitcast(E4M3_X4),
                scales=u_scales[:, s, i * H : (i + 1) * H],
                in_=u_grouped[(i, s)][:].rearrange("p w j -> p (w j)"),
            )

        def load_zn(s, half):
            js = slice(half * HALF, (half + 1) * HALF)
            nc.sync.dma_start(out=zn_sb[:, s, js, :], in_=tokens_by_pass(zn_dram)[s][:, js, :])

        def make_neg_ga(s, half):
            js = slice(half * HALF, (half + 1) * HALF)
            nc.vector.scalar_tensor_tensor(
                out=neg_ga[:, s, js], in0=zn_sb[:, s, js, 0:H], scalar=1.0, in1=g_sb[:, s, js],
                op0=ALU.subtract, op1=ALU.mult,
            )

        def make_z_factor(s, half):
            js = slice(half * HALF, (half + 1) * HALF)
            nc.vector.tensor_tensor(
                out=zn_sb[:, s, js, 0:H], in0=neg_ga[:, s, js], in1=zn_sb[:, s, js, 0:H], op=ALU.mult
            )

        def square_n(s, half):
            js = slice(half * HALF, (half + 1) * HALF)
            nc.scalar.activation(out=d_n[:, s, js], in_=zn_sb[:, s, js, H : 2 * H], func=ACT.Square)

        def make_d_n(s):
            nc.vector.scalar_tensor_tensor(
                out=d_n[:, s], in0=d_n[:, s], scalar=1.0, in1=neg_ga[:, s],
                op0=ALU.subtract, op1=ALU.mult,
            )

        def regroup_d_n(engine, s):
            grouped = wide.tile([P, H, PACK], BF16, align_bytes=64, tag="wide", name="dn_grouped")
            dn_grouped[s] = grouped
            copy_on(engine, by_runs_out(grouped[:]), by_runs_in(d_n[:, s]))

        def quantise_pass(which, s, grouped):
            nc.vector.quantize_mx(
                out=nz_codes[:, which, s, :].bitcast(E5M2_X4),
                scales=nz_scales[:, which, s, :],
                in_=grouped.rearrange("p w j -> p (w j)"),
            )

        def subtract_h(s, b):
            cols = slice(b * M_TILE, (b + 1) * M_TILE)
            bank = psum.tile([P, PACK, M_TILE], F32, tag="acc", name="n_minus_h")
            n_minus_h[(s, b)] = bank
            n_cols = slice(H + b * M_TILE, H + (b + 1) * M_TILE)
            nc.tensor.matmul(out=bank[:], lhsT=ident[:], rhs=zn_sb[:, s, :, n_cols], start=True, stop=False)
            nc.tensor.matmul(out=bank[:], lhsT=neg_ident[:], rhs=h_sb[:, s, :, cols], start=False, stop=True)

        def make_d_z(s, b):
            cols = slice(b * M_TILE, (b + 1) * M_TILE)
            nc.vector.tensor_tensor(
                out=by_runs_out(d_z_grouped[:, s, cols, :]),
                in0=by_runs_in(n_minus_h[(s, b)][:]),
                in1=by_runs_in(zn_sb[:, s, :, cols]),
                op=ALU.mult,
            )

        def square_r(s):
            nc.scalar.activation(out=r_sb[:, s], in_=r_sb[:, s], func=ACT.Square, bias=-0.5, scale=1.0)

        def times_h_n(b):
            cols = slice(b * M_TILE, (b + 1) * M_TILE)
            nc.vector.scalar_tensor_tensor(
                out=r_sb[:, :, :, cols], in0=r_sb[:, :, :, cols], scalar=0.25,
                in1=hn_sb[:, :, :, cols], op0=ALU.subtract, op1=ALU.mult,
            )

        dr_grouped = {}

        def make_d_r(b):
            cols = slice(b * M_TILE, (b + 1) * M_TILE)
            grouped = narrow.tile([P, PASSES, M_TILE, PACK], BF16, align_bytes=64, tag="narrow", name="dr_grouped")
            dr_grouped[b] = grouped
            for s in range(PASSES):
                nc.vector.scalar_tensor_tensor(
                    out=grouped[:, s],
                    in0=r_sb[:, s, :, cols].rearrange("p j w -> p w j"), scalar=-1.0,
                    in1=d_n[:, s, :, cols].rearrange("p j w -> p w j"),
                    op0=ALU.mult, op1=ALU.mult,
                )

        def quantise_d_r(b):
            nc.vector.quantize_mx(
                out=r_codes[:, b].rearrange("p s w -> p (s w)").bitcast(E5M2_X4),
                scales=r_scales[:, b].rearrange("p s w -> p (s w)"),
                in_=dr_grouped[b][:].rearrange("p s w j -> p (s w j)"),
            )

        def stationary(gate, b, s):
            cols = slice(b * M_TILE, (b + 1) * M_TILE)
            if gate == R_GATE:
                return r_codes[:, b, s, :], r_scales[:, b, s, :]
            which = 0 if gate == N_GATE else 1
            return nz_codes[:, which, s, cols], nz_scales[:, which, s, cols]

        def multiply(gate, b, i):
            bank = psum.tile([P, H], F32, tag="acc", name="acc")
            acc[(gate, b, i)] = bank
            for s in range(PASSES):
                codes, scales = stationary(gate, b, s)
                nc.tensor.matmul_mx(
                    out=bank[:],
                    lhsT=codes.bitcast(E5M2_X4),
                    lhsT_scale=scales,
                    rhs=u_codes[:, s, i * H : (i + 1) * H].bitcast(E4M3_X4),
                    rhs_scale=u_scales[:, s, i * H : (i + 1) * H],
                    start=(s == 0),
                    stop=(s == PASSES - 1),
                )

        def empty(engine, gate, b, i):
            if (gate, b) not in rows:
                rows[(gate, b)] = stage.tile([P, STREAMS * H], F32, tag="rows", name="rows")
            copy_on(engine, rows[(gate, b)][:, i * H : (i + 1) * H], acc[(gate, b, i)][:])

        def store(gate, b):
            m = gate * TILES_PER_GATE + b
            nc.sync.dma_start(out=out[m * M_TILE : (m + 1) * M_TILE, :], in_=rows[(gate, b)][:])

        def last_row_tile(gate, b, engines):
            m = gate * TILES_PER_GATE + b
            for i in range(STREAMS):
                multiply(gate, b, i)
            for i in range(STREAMS):
                empty(engines[i], gate, b, i)
                nc.sync.dma_start(
                    out=out[m * M_TILE : (m + 1) * M_TILE, i * H : (i + 1) * H],
                    in_=rows[(gate, b)][:, i * H : (i + 1) * H],
                )

        def row_tile(gate, b, engines):
            for i in range(STREAMS):
                multiply(gate, b, i)
            for i in range(STREAMS):
                empty(engines[i], gate, b, i)
            store(gate, b)

        with tc.manual_schedule():
            make_identity(nc, ident[:])
            nc.scalar.mul(out=neg_ident[:], in_=ident[:], mul=-1.0)

            load_u(X, 0)
            load_u(X, 1)
            load_u(Z, 0)
            load(g_sb, grad_out, 0)
            load_zn(0, 0)
            load_zn(0, 1)
            load(h_sb, h_prev, 0)
            load_u(Z, 1)
            load(g_sb, grad_out, 1)
            load_zn(1, 0)
            load_zn(1, 1)
            load(h_sb, h_prev, 1)
            load_u(A, 0)
            load_u(A, 1)
            load(r_sb, r_dram, 0)
            load(r_sb, r_dram, 1)
            load(hn_sb, h_n, 0)
            load(hn_sb, h_n, 1)

            regroup_u("V", X, 0)
            regroup_u("S", X, 1)
            quantise_u(X, 0)
            regroup_u("V", Z, 0)
            quantise_u(X, 1)
            quantise_u(Z, 0)
            for half in range(2):
                make_neg_ga(0, half)
                square_n(0, half)
                make_z_factor(0, half)
            for b in range(TILES_PER_GATE):
                subtract_h(0, b)
            regroup_u("S", Z, 1)
            make_d_n(0)
            regroup_d_n("S", 0)
            make_d_z(0, 0)
            quantise_u(Z, 1)
            make_neg_ga(1, 0)
            square_n(1, 0)
            quantise_pass(0, 0, dn_grouped[0][:])
            make_z_factor(1, 0)
            make_neg_ga(1, 1)
            square_n(1, 1)
            make_z_factor(1, 1)
            for b in range(TILES_PER_GATE):
                subtract_h(1, b)
            regroup_u("S", A, 0)
            make_d_n(1)
            regroup_u("S", A, 1)
            quantise_u(A, 0)
            regroup_d_n("V", 1)
            quantise_u(A, 1)
            quantise_pass(0, 1, dn_grouped[1][:])
            square_r(0)

            make_d_z(0, 1)
            make_d_z(0, 2)
            for i in range(STREAMS):
                multiply(N_GATE, 0, i)
            make_d_z(0, 3)
            make_d_z(1, 0)
            make_d_z(1, 1)
            for i in range(STREAMS):
                empty("S", N_GATE, 0, i)
            store(N_GATE, 0)
            for i in range(STREAMS):
                multiply(N_GATE, 1, i)
            make_d_z(1, 2)
            make_d_z(1, 3)
            for i in range(STREAMS):
                empty("S", N_GATE, 1, i)
            store(N_GATE, 1)
            quantise_pass(1, 0, d_z_grouped[:, 0])
            quantise_pass(1, 1, d_z_grouped[:, 1])
            row_tile(N_GATE, 2, "SSV")
            row_tile(N_GATE, 3, "VVV")
            square_r(1)
            times_h_n(0)
            times_h_n(1)
            row_tile(Z_GATE, 0, "SSS")
            make_d_r(0)
            make_d_r(1)
            quantise_d_r(0)
            row_tile(Z_GATE, 1, "SSS")
            times_h_n(2)
            quantise_d_r(1)
            row_tile(Z_GATE, 2, "SSS")
            make_d_r(2)
            times_h_n(3)
            quantise_d_r(2)
            row_tile(Z_GATE, 3, "SSS")
            row_tile(R_GATE, 0, "SSS")
            make_d_r(3)
            quantise_d_r(3)
            row_tile(R_GATE, 1, "SSS")
            row_tile(R_GATE, 2, "SSV")
            last_row_tile(R_GATE, 3, "SVS")
